import numpy as np
import ml_dtypes


def mxq(x, axis, fmt="e4m3"):
    dtype, down = {"e4m3": (ml_dtypes.float8_e4m3fn, 7), "e5m2": (ml_dtypes.float8_e5m2, 14)}[fmt]
    v = np.moveaxis(np.asarray(x, np.float32).astype(ml_dtypes.bfloat16).astype(np.float64), axis, -1)
    blocks = v.reshape(v.shape[:-1] + (-1, 32))
    amax = np.abs(blocks).max(-1, keepdims=True)
    byte = np.maximum(np.where(amax > 0, np.frexp(amax)[1] - 1 + 127, 0) - down, 1)
    scale = np.exp2(byte - 127.0)
    codes = (blocks / scale).astype(np.float32).astype(dtype).astype(np.float64)
    return np.moveaxis((codes * scale).reshape(v.shape), -1, axis)


WIDE = False


def mx_kscale(k):
    if not WIDE:
        return np.ones(k)
    levels = np.array([30, -30])
    if k % 512:
        return np.exp2(np.random.permutation(np.resize(levels, k // 32))).repeat(32)
    a = np.empty((k // 512, 16))
    for p in range(k // 512):
        a[p, :8] = np.random.permutation(np.resize(levels, 8))
        for g in range(8):
            far = levels[np.abs(levels - a[p, g]) >= 10]
            a[p, g + 8] = far[np.random.randint(len(far))]
    return np.exp2(a.ravel()).repeat(32)


BF16 = ml_dtypes.bfloat16


def bf(x):
    return np.asarray(x, np.float32).astype(BF16)


def f64(x):
    return np.asarray(x).astype(np.float64)


B, N, DI, D, H, DO = 2, 512, 1024, 1024, 16, 1024
DH = D // H
SIG = 0.5


def time_concat(space):
    t = np.sqrt(1.0 + np.sum(space * space, axis=-1, keepdims=True))
    return np.concatenate([t, space], axis=-1)


def split_lift(space):
    return time_concat(space.reshape(B, N, H, DH).transpose(0, 2, 1, 3))


def setup_inputs():
    s = mx_kscale(DI)
    return {"x_space": bf(np.random.standard_normal((B, N, DI)) * s),
            "Wq": bf(np.random.standard_normal((D, DI)) * SIG / np.sqrt(DI) / s),
            "bq": bf(np.random.standard_normal(D) * 0.1),
            "Wk": bf(np.random.standard_normal((D, DI)) * SIG / np.sqrt(DI) / s),
            "bk": bf(np.random.standard_normal(D) * 0.1)}


def reference(x_space, Wq, bq, Wk, bk):
    xq = mxq(f64(x_space), 2, "e5m2")
    q = (xq @ mxq(f64(Wq), 1, "e4m3").T) + f64(bq)
    k = (xq @ mxq(f64(Wk), 1, "e4m3").T) + f64(bk)
    return split_lift(q), split_lift(k)

@@ -1,0 +1,287 @@
+from contextlib import ExitStack
+
+import concourse.mybir as mybir
+from concourse.masks import make_identity
+
+B, N, DI, D, H = 2, 512, 1024, 1024, 16
+DH = D // H
+FLOPS = 2 * B * N * DI * 2 * D
+
+F32 = mybir.dt.float32
+BF16 = mybir.dt.bfloat16
+I32 = mybir.dt.int32
+U32 = mybir.dt.uint32
+U8 = mybir.dt.uint8
+E4M3 = mybir.dt.float8_e4m3fn_x4
+E5M2 = mybir.dt.float8_e5m2_x4
+ALU = mybir.AluOpType
+ACT = mybir.ActivationFunctionType
+
+P = 128
+TOK = 8
+PASSES = 2
+PASS_WORDS = 256
+HEADS = 4
+FEATS = HEADS * DH
+CHUNKS = 2 * D // FEATS
+BANKS = TOK // 2
+ROW = DH + 1
+VEC_GROUPS = 12
+
+
+def tile_lorentzmultiheadattention_pa_kernel(tc, x_space, Wq, bq, Wk, bk, out_0, out_1):
+    nc = tc.nc
+    with ExitStack() as ctx:
+        keep = ctx.enter_context(tc.tile_pool(name="keep", bufs=1))
+        work = ctx.enter_context(tc.tile_pool(name="work", bufs=3))
+        psum = ctx.enter_context(tc.psum_pool(name="psum", bufs=1))
+        ctx.enter_context(tc.manual_schedule())
+
+        bias_rows = keep.tile([P, 512], BF16, name="bias_rows")
+        nc.gpsimd.memset(bias_rows[:].bitcast(I32), 0)
+        ident = keep.tile([P, P], F32, name="ident")
+        make_identity(nc, ident[:])
+
+        x_view = x_space.rearrange("b (g j) k -> g b j k", j=TOK)
+        x_raw = {}
+        w_raw = {}
+
+        def load_x(j0, count):
+            t = keep.tile([P, count, DI], BF16, name="x_raw%d" % j0)
+            nc.sync.dma_start(out=t[:], in_=x_view[:, :, j0:j0 + count, :])
+            for j in range(count):
+                x_raw[j0 + j] = t[:, j, :]
+
+        def load_w(c):
+            W = Wq if c < CHUNKS // 2 else Wk
+            f0 = (c % (CHUNKS // 2)) * FEATS
+            t = keep.tile([P, 2, DI], BF16, name="w_raw%d" % c)
+            nc.sync.dma_start(out=t[:], in_=W[f0:f0 + FEATS, :].rearrange("(r i) k -> r i k", i=2))
+            w_raw[c] = t
+
+        load_x(0, 1)
+        nc.sync.dma_start(out=bias_rows[0:2, :], in_=bq.rearrange("(r n) -> r n", r=2))
+        nc.sync.dma_start(out=bias_rows[2:4, :], in_=bk.rearrange("(r n) -> r n", r=2))
+        load_w(0)
+        load_x(1, 1)
+        for j0 in range(2, TOK, 2):
+            load_x(j0, 2)
+        for c in range(1, CHUNKS):
+            load_w(c)
+
+        select = keep.tile([P, 4], BF16, name="select")
+        nc.scalar.activation(out=select[:], in_=ident[:, 0:4], func=ACT.Sqrt)
+        bias = keep.tile([P, 2, D], BF16, name="bias")
+
+        def spread_bias():
+            for m in range(2):
+                bank = psum.tile([P, 2, 512], BF16, name="bias_bank", tag="mm", bufs=5)
+                for r in range(2):
+                    nc.tensor.matmul(bank[:, r, :], lhsT=select[:, 2 * m + r:2 * m + r + 1].to_broadcast([P, P]),
+                                     rhs=bias_rows[:], start=True, stop=True)
+                if m == 0:
+                    nc.vector.tensor_copy(out=bias[:, m, :], in_=bank[:].rearrange("p r n -> p (r n)"))
+                else:
+                    nc.scalar.copy(out=bias[:, m, :], in_=bank[:].rearrange("p r n -> p (r n)"))
+
+        x_codes = [keep.tile([P, 2, PASSES, P], U32, name="x_codes%d" % q, align_bytes=64) for q in range(BANKS)]
+        x_scales = [keep.tile([P, 2, PASSES, P], U8, name="x_scales%d" % q, align_bytes=64) for q in range(BANKS)]
+        w_codes = [keep.tile([P, PASSES, FEATS], U32, name="w_codes%d" % c, align_bytes=64) for c in range(CHUNKS)]
+        w_scales = [keep.tile([P, PASSES, FEATS], U8, name="w_scales%d" % c, align_bytes=64) for c in range(CHUNKS)]
+        stage = [keep.tile([P, HEADS, TOK, ROW], F32, name="stage%d" % c) for c in range(CHUNKS)]
+
+        def new_grouped():
+            return work.tile([P, 2, 512], F32, name="grouped", tag="grouped", bufs=3, align_bytes=64)
+
+        def transpose_x(j):
+            bank = psum.tile([P, PASSES, 2, P], F32, name="tr_bank", tag="tr", bufs=3)
+            words = x_raw[j].bitcast(F32)
+            for g in range(PASSES):
+                for u in range(2):
+                    nc.tensor.transpose(bank[:, g, u, :], words[:, PASS_WORDS * g + u:PASS_WORDS * (g + 1):2], ident[:])
+            return bank
+
+        def transpose_w(c, g):
+            bank = psum.tile([P, 2, 2, P], F32, name="tr_bank", tag="tr", bufs=3)
+            for i in range(2):
+                words = w_raw[c][:, i, :].bitcast(F32)
+                for u in range(2):
+                    nc.tensor.transpose(bank[:, i, u, :], words[:, PASS_WORDS * g + u:PASS_WORDS * (g + 1):2], ident[:])
+            return bank
+
+        def copy(on_vector, out, in_):
+            if on_vector:
+                nc.vector.tensor_copy(out=out, in_=in_)
+            else:
+                nc.scalar.copy(out=out, in_=in_)
+
+        def copy_x(bank, grouped, half, on_vector=False):
+            copy(on_vector, grouped[:, half, :].rearrange("p (g r u) -> p g r u", g=PASSES, u=2),
+                 bank[:].rearrange("p g u r -> p g r u"))
+
+        def copy_w(bank, grouped, g, on_vector=False):
+            copy(on_vector, grouped[:, g, :].rearrange("p (r s) -> p r s", s=4),
+                 bank[:].rearrange("p i u r -> p r (i u)"))
+
+        def quantize_x(q, grouped, lo=0, hi=2):
+            nc.vector.quantize_mx(
+                out=x_codes[q][:, lo:hi].rearrange("p j g r -> p (j g r)").bitcast(E5M2),
+                scales=x_scales[q][:, lo:hi].rearrange("p j g r -> p (j g r)"),
+                in_=grouped[:, lo:hi, :].rearrange("p a w -> p (a w)").bitcast(BF16))
+
+        def quantize_w(c, grouped):
+            nc.vector.quantize_mx(
+                out=w_codes[c][:].rearrange("p g n -> p (g n)").bitcast(E4M3),
+                scales=w_scales[c][:].rearrange("p g n -> p (g n)"),
+                in_=grouped[:].rearrange("p a w -> p (a w)").bitcast(BF16))
+
+        units = [(c, 0, HEADS, VEC_GROUPS) for c in range(CHUNKS - 1)]
+        units += [(CHUNKS - 1, 0, 2, TOK), (CHUNKS - 1, 2, 2, TOK)]
+        steps = []
+        for u, (c, h0, nh, nv) in enumerate(units):
+            nj = 512 // (nh * DH)
+            steps += [(u, j0, nj) for j0 in range(0, TOK, nj)]
+        STEPS = len(steps)
+
+        products = {}
+        sums = {}
+        stats = {}
+        squares = {}
+        mean_sq = {}
+
+        def multiply(s):
+            u, j0, nj = steps[s]
+            c, h0, nh, nv = units[u]
+            cols = slice(h0 * DH, (h0 + nh) * DH)
+            bank = psum.tile([P, nj, nh * DH], F32, name="mm_bank", tag="mm", bufs=5)
+            for jj in range(nj):
+                q, half = divmod(j0 + jj, 2)
+                for g in range(PASSES):
+                    nc.tensor.matmul_mx(
+                        out=bank[:, jj, :],
+                        lhsT=x_codes[q][:, half, g, :].bitcast(E5M2), lhsT_scale=x_scales[q][:, half, g, :],
+                        rhs=w_codes[c][:, g, cols].bitcast(E4M3), rhs_scale=w_scales[c][:, g, cols],
+                        start=(g == 0), stop=(g == PASSES - 1))
+            products[s] = bank
+
+        def add_bias(s):
+            u, j0, nj = steps[s]
+            c, h0, nh, nv = units[u]
+            f0 = (c % (CHUNKS // 2)) * FEATS + h0 * DH
+            b = bias[:, c // (CHUNKS // 2), f0:f0 + nh * DH].rearrange("p (h d) -> p h d", d=DH)
+            nc.vector.tensor_tensor(
+                out=stage[c][:, h0:h0 + nh, j0:j0 + nj, 1:ROW],
+                in0=products[s][:].rearrange("p j (h d) -> p h j d", d=DH),
+                in1=b.unsqueeze(2).to_broadcast([P, nh, nj, DH]),
+                op=ALU.add)
+
+        def open_sums(u):
+            c, h0, nh, nv = units[u]
+            sums[u] = work.tile([P, nh * TOK], F32, name="sums", tag="sums", bufs=3)
+            stats[u] = work.tile([P, nv, 3], F32, name="stats", tag="stats", bufs=3)
+            mean_sq[u] = work.tile([P, nv], F32, name="mean_sq", tag="mean_sq", bufs=3)
+            squares[u] = work.tile([P, nh * TOK, DH], BF16, name="squares", tag="squares", bufs=2)
+
+        def sums_vector(s):
+            u, j0, nj = steps[s]
+            c, h0, nh, nv = units[u]
+            if j0 == 0:
+                open_sums(u)
+            for h in range(nh):
+                for j in range(j0, j0 + nj, 2):
+                    col = h * TOK + j
+                    if col < nv:
+                        nc.vector.bn_stats(
+                            out=stats[u][:, col:col + 2, :].rearrange("p a s -> p (a s)"),
+                            in_=stage[c][:, h0 + h, j:j + 2, 1:ROW].rearrange("p j d -> p d j"))
+
+        def sums_scalar(s):
+            u, j0, nj = steps[s]
+            c, h0, nh, nv = units[u]
+            for h in range(nh):
+                for j in range(j0, j0 + nj):
+                    col = h * TOK + j
+                    if col >= nv:
+                        nc.scalar.activation(out=squares[u][:, col, :], in_=stage[c][:, h0 + h, j, 1:ROW],
+                                             func=ACT.Square, accum_out=sums[u][:, col:col + 1])
+
+        def post_mean(u):
+            nc.vector.scalar_tensor_tensor(out=mean_sq[u][:], in0=stats[u][:, :, 1], scalar=float(DH),
+                                           in1=stats[u][:, :, 1], op0=ALU.mult, op1=ALU.mult)
+
+        def post_sum(u):
+            nc.vector.tensor_tensor(out=sums[u][:, 0:units[u][3]], in0=mean_sq[u][:], in1=stats[u][:, :, 2], op=ALU.add)
+
+        def lift_and_store(u):
+            c, h0, nh, nv = units[u]
+            nc.scalar.activation(out=stage[c][:, h0:h0 + nh, :, 0].rearrange("p h j -> p (h j)"), in_=sums[u][:],
+                                 func=ACT.Sqrt, bias=1.0)
+            out = out_0 if c < CHUNKS // 2 else out_1
+            view = out.rearrange("b h (g j) c -> h g b (j c)", j=TOK)
+            first = (c % (CHUNKS // 2)) * HEADS
+            for h in range(h0, h0 + nh):
+                nc.sync.dma_start(out=view[first + h], in_=stage[c][:, h].rearrange("p j c -> p (j c)"))
+
+        def closes(s):
+            return 0 <= s < STEPS and steps[s][1] + steps[s][2] == TOK
+
+        gx = new_grouped()
+        gw = new_grouped()
+        copy_x(transpose_x(0), gx, 0)
+        spread_bias()
+        quantize_x(0, gx, 0, 1)
+        copy_w(transpose_w(0, 0), gw, 0, on_vector=True)
+        copy_w(transpose_w(0, 1), gw, 1)
+        copy_x(transpose_x(1), gx, 1, on_vector=True)
+        quantize_w(0, gw)
+        quantize_x(0, gx, 1, 2)
+        for q in range(1, BANKS):
+            gx = new_grouped()
+            copy_x(transpose_x(2 * q), gx, 0)
+            copy_x(transpose_x(2 * q + 1), gx, 1)
+            multiply(q - 1)
+            add_bias(q - 1)
+            quantize_x(q, gx)
+            if q >= 2:
+                sums_vector(q - 2)
+                sums_scalar(q - 2)
+        gw = new_grouped()
+        copy_w(transpose_w(1, 0), gw, 0)
+        copy_w(transpose_w(1, 1), gw, 1)
+        multiply(BANKS - 1)
+        add_bias(BANKS - 1)
+        quantize_w(1, gw)
+        sums_vector(BANKS - 2)
+        gw = new_grouped()
+        copy_w(transpose_w(2, 0), gw, 0)
+        copy_w(transpose_w(2, 1), gw, 1)
+        sums_scalar(BANKS - 2)
+        for q in range(BANKS):
+            multiply(BANKS + q)
+
+        for s in range(BANKS, STEPS + 3):
+            c, q = divmod(s, BANKS)
+            more = c + 2 < CHUNKS
+            if s < STEPS:
+                add_bias(s)
+            if s == BANKS:
+                quantize_w(2, gw)
+            if more and q == 0:
+                gw = new_grouped()
+                banks = [transpose_w(c + 2, g) for g in range(PASSES)]
+            if s + BANKS < STEPS:
+                multiply(s + BANKS)
+            if closes(s - 2):
+                post_mean(steps[s - 2][0])
+            if s - 1 < STEPS:
+                sums_vector(s - 1)
+            if closes(s - 2):
+                post_sum(steps[s - 2][0])
+            if closes(s - 3):
+                lift_and_store(steps[s - 3][0])
+            if s - 1 < STEPS:
+                sums_scalar(s - 1)
+            if more and q < PASSES:
+                copy_w(banks[q], gw, q)
+            if more and q == BANKS - 1:
+                quantize_w(c + 2, gw)

@@ -18,15 +18,19 @@ ALU = mybir.AluOpType
 ACT = mybir.ActivationFunctionType
 
 P = 128
-TOK = 8
+BANK = 512
+TILES = 8
 PASSES = 2
-PASS_WORDS = 256
+PASS_PAIRS = 256
+ROW = DH + 1
 HEADS = 4
 FEATS = HEADS * DH
 CHUNKS = 2 * D // FEATS
-BANKS = TOK // 2
-ROW = DH + 1
-VEC_GROUPS = 12
+CHUNK_STEPS = TILES * FEATS // BANK
+TRANSPOSE_BANKS, PRODUCT_BANKS = 3, 5
+HALVED_CHUNKS = 2
+VECTOR_EIGHTHS = 3
+WEIGHT_LEAD = 5
 
 
 def tile_lorentzmultiheadattention_pa_kernel(tc, x_space, Wq, bq, Wk, bk, out_0, out_1):
@@ -37,77 +41,66 @@ def tile_lorentzmultiheadattention_pa_kernel(tc, x_space, Wq, bq, Wk, bk, out_0,
         psum = ctx.enter_context(tc.psum_pool(name="psum", bufs=1))
         ctx.enter_context(tc.manual_schedule())
 
-        bias_rows = keep.tile([P, 512], BF16, name="bias_rows")
-        nc.gpsimd.memset(bias_rows[:].bitcast(I32), 0)
+        bq_rows = keep.tile([P, BANK], BF16, name="bq_rows")
+        nc.gpsimd.memset(bq_rows[:].bitcast(I32), 0)
         ident = keep.tile([P, P], F32, name="ident")
         make_identity(nc, ident[:])
+        shuffle = keep.tile([P, P], F32, name="shuffle")
+        nc.vector.tensor_copy(out=shuffle[:].rearrange("p (a b) -> p a b", b=B),
+                              in_=ident[:].rearrange("p (b a) -> p a b", b=B))
 
-        x_view = x_space.rearrange("b (g j) k -> g b j k", j=TOK)
-        x_raw = {}
-        w_raw = {}
+        def every_second_pair(row):
+            pairs = row.bitcast(F32)
+            return [[pairs[:, PASS_PAIRS * g + u:PASS_PAIRS * (g + 1):2] for u in range(2)] for g in range(PASSES)]
+
+        x_rows = x_space.rearrange("b (a j) k -> (b a) j k", j=TILES)
+        x_pairs = {}
+        w_pairs = {}
 
         def load_x(j0, count):
-            t = keep.tile([P, count, DI], BF16, name="x_raw%d" % j0)
-            nc.sync.dma_start(out=t[:], in_=x_view[:, :, j0:j0 + count, :])
+            raw = keep.tile([P, count, DI], BF16, name="x_raw%d" % j0)
+            nc.sync.dma_start(out=raw[:], in_=x_rows[:, j0:j0 + count, :])
             for j in range(count):
-                x_raw[j0 + j] = t[:, j, :]
+                x_pairs[j0 + j] = every_second_pair(raw[:, j, :])
 
         def load_w(c):
-            W = Wq if c < CHUNKS // 2 else Wk
-            f0 = (c % (CHUNKS // 2)) * FEATS
-            t = keep.tile([P, 2, DI], BF16, name="w_raw%d" % c)
-            nc.sync.dma_start(out=t[:], in_=W[f0:f0 + FEATS, :].rearrange("(r i) k -> r i k", i=2))
-            w_raw[c] = t
+            weights = Wq if c < CHUNKS // 2 else Wk
+            f0 = c * FEATS % D
+            raw = keep.tile([P, 2, DI], BF16, name="w_raw%d" % c)
+            nc.sync.dma_start(out=raw[:], in_=weights[f0:f0 + FEATS, :].rearrange("(r i) k -> r i k", i=2))
+            w_pairs[c] = [every_second_pair(raw[:, i, :]) for i in range(2)]
 
         load_x(0, 1)
-        nc.sync.dma_start(out=bias_rows[0:2, :], in_=bq.rearrange("(r n) -> r n", r=2))
-        nc.sync.dma_start(out=bias_rows[2:4, :], in_=bk.rearrange("(r n) -> r n", r=2))
+        nc.sync.dma_start(out=bq_rows[0:2, :], in_=bq.rearrange("(r n) -> r n", r=2))
         load_w(0)
         load_x(1, 1)
-        for j0 in range(2, TOK, 2):
+        load_w(1)
+        for j0 in range(2, TILES, 2):
             load_x(j0, 2)
-        for c in range(1, CHUNKS):
+        for c in range(2, CHUNKS):
             load_w(c)
+        bias_k = keep.tile([P, D], BF16, name="bias_k")
+        nc.sync.dma_start(out=bias_k[:], in_=bk.partition_broadcast(P))
 
-        select = keep.tile([P, 4], BF16, name="select")
-        nc.scalar.activation(out=select[:], in_=ident[:, 0:4], func=ACT.Sqrt)
-        bias = keep.tile([P, 2, D], BF16, name="bias")
+        select = keep.tile([P, 2], BF16, name="select")
+        nc.scalar.activation(out=select[:], in_=ident[:, 0:2], func=ACT.Sqrt)
+        bias_q = keep.tile([P, D], BF16, name="bias_q")
 
-        def spread_bias():
-            for m in range(2):
-                bank = psum.tile([P, 2, 512], BF16, name="bias_bank", tag="mm", bufs=5)
-                for r in range(2):
-                    nc.tensor.matmul(bank[:, r, :], lhsT=select[:, 2 * m + r:2 * m + r + 1].to_broadcast([P, P]),
-                                     rhs=bias_rows[:], start=True, stop=True)
-                if m == 0:
-                    nc.vector.tensor_copy(out=bias[:, m, :], in_=bank[:].rearrange("p r n -> p (r n)"))
-                else:
-                    nc.scalar.copy(out=bias[:, m, :], in_=bank[:].rearrange("p r n -> p (r n)"))
+        def spread_bq():
+            bank = psum.tile([P, 2, BANK], BF16, name="bq_bank", tag="product", bufs=PRODUCT_BANKS)
+            for r in range(2):
+                nc.tensor.matmul(bank[:, r, :], lhsT=select[:, r:r + 1].to_broadcast([P, P]), rhs=bq_rows[:],
+                                 start=True, stop=True)
+            nc.scalar.copy(out=bias_q[:], in_=bank[:].rearrange("p r n -> p (r n)"))
 
-        x_codes = [keep.tile([P, 2, PASSES, P], U32, name="x_codes%d" % q, align_bytes=64) for q in range(BANKS)]
-        x_scales = [keep.tile([P, 2, PASSES, P], U8, name="x_scales%d" % q, align_bytes=64) for q in range(BANKS)]
+        x_codes = [keep.tile([P, 2, PASSES, P], U32, name="x_codes%d" % q, align_bytes=64) for q in range(TILES // 2)]
+        x_scales = [keep.tile([P, 2, PASSES, P], U8, name="x_scales%d" % q, align_bytes=64) for q in range(TILES // 2)]
         w_codes = [keep.tile([P, PASSES, FEATS], U32, name="w_codes%d" % c, align_bytes=64) for c in range(CHUNKS)]
         w_scales = [keep.tile([P, PASSES, FEATS], U8, name="w_scales%d" % c, align_bytes=64) for c in range(CHUNKS)]
-        stage = [keep.tile([P, HEADS, TOK, ROW], F32, name="stage%d" % c) for c in range(CHUNKS)]
+        stage = [keep.tile([P, HEADS, TILES, ROW], F32, name="stage%d" % c) for c in range(CHUNKS)]
 
         def new_grouped():
-            return work.tile([P, 2, 512], F32, name="grouped", tag="grouped", bufs=3, align_bytes=64)
-
-        def transpose_x(j):
-            bank = psum.tile([P, PASSES, 2, P], F32, name="tr_bank", tag="tr", bufs=3)
-            words = x_raw[j].bitcast(F32)
-            for g in range(PASSES):
-                for u in range(2):
-                    nc.tensor.transpose(bank[:, g, u, :], words[:, PASS_WORDS * g + u:PASS_WORDS * (g + 1):2], ident[:])
-            return bank
-
-        def transpose_w(c, g):
-            bank = psum.tile([P, 2, 2, P], F32, name="tr_bank", tag="tr", bufs=3)
-            for i in range(2):
-                words = w_raw[c][:, i, :].bitcast(F32)
-                for u in range(2):
-                    nc.tensor.transpose(bank[:, i, u, :], words[:, PASS_WORDS * g + u:PASS_WORDS * (g + 1):2], ident[:])
-            return bank
+            return work.tile([P, 2, BANK], F32, name="grouped", tag="grouped", bufs=4, align_bytes=64)
 
         def copy(on_vector, out, in_):
             if on_vector:
@@ -115,46 +108,65 @@ def tile_lorentzmultiheadattention_pa_kernel(tc, x_space, Wq, bq, Wk, bk, out_0,
             else:
                 nc.scalar.copy(out=out, in_=in_)
 
-        def copy_x(bank, grouped, half, on_vector=False):
-            copy(on_vector, grouped[:, half, :].rearrange("p (g r u) -> p g r u", g=PASSES, u=2),
-                 bank[:].rearrange("p g u r -> p g r u"))
+        def turn_x(j, grouped, on_vector):
+            bank = psum.tile([P, PASSES, 2, P], F32, name="x_bank", tag="transpose", bufs=TRANSPOSE_BANKS)
+            for g in range(PASSES):
+                for u in range(2):
+                    nc.tensor.transpose(bank[:, g, u, :], x_pairs[j][g][u], shuffle[:])
+            copy(on_vector, grouped[:, j % 2, :].rearrange("p (g m u) -> p g m u", g=PASSES, u=2),
+                 bank[:].rearrange("p g u m -> p g m u"))
 
-        def copy_w(bank, grouped, g, on_vector=False):
-            copy(on_vector, grouped[:, g, :].rearrange("p (r s) -> p r s", s=4),
+        def turn_w(c, g, grouped, on_vector):
+            bank = psum.tile([P, 2, 2, P], F32, name="w_bank", tag="transpose", bufs=TRANSPOSE_BANKS)
+            for i in range(2):
+                for u in range(2):
+                    nc.tensor.transpose(bank[:, i, u, :], w_pairs[c][i][g][u], ident[:])
+            copy(on_vector, grouped[:, g, :].rearrange("p (r iu) -> p r iu", iu=4),
                  bank[:].rearrange("p i u r -> p r (i u)"))
 
-        def quantize_x(q, grouped, lo=0, hi=2):
+        def quantize_x(q, grouped, lo, hi):
             nc.vector.quantize_mx(
-                out=x_codes[q][:, lo:hi].rearrange("p j g r -> p (j g r)").bitcast(E5M2),
-                scales=x_scales[q][:, lo:hi].rearrange("p j g r -> p (j g r)"),
-                in_=grouped[:, lo:hi, :].rearrange("p a w -> p (a w)").bitcast(BF16))
+                out=x_codes[q][:, lo:hi].rearrange("p j g m -> p (j g m)").bitcast(E5M2),
+                scales=x_scales[q][:, lo:hi].rearrange("p j g m -> p (j g m)"),
+                in_=grouped[:, lo:hi, :].rearrange("p j w -> p (j w)").bitcast(BF16))
 
         def quantize_w(c, grouped):
             nc.vector.quantize_mx(
                 out=w_codes[c][:].rearrange("p g n -> p (g n)").bitcast(E4M3),
                 scales=w_scales[c][:].rearrange("p g n -> p (g n)"),
-                in_=grouped[:].rearrange("p a w -> p (a w)").bitcast(BF16))
+                in_=grouped[:].rearrange("p g w -> p (g w)").bitcast(BF16))
 
-        units = [(c, 0, HEADS, VEC_GROUPS) for c in range(CHUNKS - 1)]
-        units += [(CHUNKS - 1, 0, 2, TOK), (CHUNKS - 1, 2, 2, TOK)]
+        def prepare_x(q):
+            grouped = new_grouped()
+            for j in (2 * q, 2 * q + 1):
+                turn_x(j, grouped, on_vector=False)
+            return lambda: quantize_x(q, grouped, 0, 2)
+
+        def prepare_w(c, vector_pass=None):
+            grouped = new_grouped()
+            for g in range(PASSES):
+                turn_w(c, g, grouped, on_vector=g == vector_pass)
+            return lambda: quantize_w(c, grouped)
+
+        units = [(c, 0, HEADS) for c in range(CHUNKS - HALVED_CHUNKS)]
+        units += [(c, h0, HEADS // 2) for c in range(CHUNKS - HALVED_CHUNKS, CHUNKS) for h0 in (0, HEADS // 2)]
         steps = []
-        for u, (c, h0, nh, nv) in enumerate(units):
-            nj = 512 // (nh * DH)
-            steps += [(u, j0, nj) for j0 in range(0, TOK, nj)]
-        STEPS = len(steps)
+        for unit, (c, h0, heads) in enumerate(units):
+            tiles = BANK // (heads * DH)
+            steps += [(unit, j0, tiles) for j0 in range(0, TILES, tiles)]
+        steps = [steps[CHUNK_STEPS * c + q] for q in range(CHUNK_STEPS) for c in range(2)] + steps[2 * CHUNK_STEPS:]
 
         products = {}
         sums = {}
         stats = {}
         squares = {}
-        mean_sq = {}
 
         def multiply(s):
-            u, j0, nj = steps[s]
-            c, h0, nh, nv = units[u]
-            cols = slice(h0 * DH, (h0 + nh) * DH)
-            bank = psum.tile([P, nj, nh * DH], F32, name="mm_bank", tag="mm", bufs=5)
-            for jj in range(nj):
+            unit, j0, tiles = steps[s]
+            c, h0, heads = units[unit]
+            cols = slice(h0 * DH, (h0 + heads) * DH)
+            bank = psum.tile([P, tiles, heads * DH], F32, name="product_bank", tag="product", bufs=PRODUCT_BANKS)
+            for jj in range(tiles):
                 q, half = divmod(j0 + jj, 2)
                 for g in range(PASSES):
                     nc.tensor.matmul_mx(
@@ -165,123 +177,100 @@ def tile_lorentzmultiheadattention_pa_kernel(tc, x_space, Wq, bq, Wk, bk, out_0,
             products[s] = bank
 
         def add_bias(s):
-            u, j0, nj = steps[s]
-            c, h0, nh, nv = units[u]
-            f0 = (c % (CHUNKS // 2)) * FEATS + h0 * DH
-            b = bias[:, c // (CHUNKS // 2), f0:f0 + nh * DH].rearrange("p (h d) -> p h d", d=DH)
+            unit, j0, tiles = steps[s]
+            c, h0, heads = units[unit]
+            f0 = c * FEATS % D + h0 * DH
+            bias = (bias_q if c < CHUNKS // 2 else bias_k)[:, f0:f0 + heads * DH].rearrange("p (h d) -> p h d", d=DH)
             nc.vector.tensor_tensor(
-                out=stage[c][:, h0:h0 + nh, j0:j0 + nj, 1:ROW],
+                out=stage[c][:, h0:h0 + heads, j0:j0 + tiles, 1:ROW],
                 in0=products[s][:].rearrange("p j (h d) -> p h j d", d=DH),
-                in1=b.unsqueeze(2).to_broadcast([P, nh, nj, DH]),
+                in1=bias.unsqueeze(2).to_broadcast([P, heads, tiles, DH]),
                 op=ALU.add)
 
-        def open_sums(u):
-            c, h0, nh, nv = units[u]
-            sums[u] = work.tile([P, nh * TOK], F32, name="sums", tag="sums", bufs=3)
-            stats[u] = work.tile([P, nv, 3], F32, name="stats", tag="stats", bufs=3)
-            mean_sq[u] = work.tile([P, nv], F32, name="mean_sq", tag="mean_sq", bufs=3)
-            squares[u] = work.tile([P, nh * TOK, DH], BF16, name="squares", tag="squares", bufs=2)
+        def vector_sums(unit):
+            return units[unit][2] * VECTOR_EIGHTHS
 
         def sums_vector(s):
-            u, j0, nj = steps[s]
-            c, h0, nh, nv = units[u]
+            unit, j0, tiles = steps[s]
+            c, h0, heads = units[unit]
             if j0 == 0:
-                open_sums(u)
-            for h in range(nh):
-                for j in range(j0, j0 + nj, 2):
-                    col = h * TOK + j
-                    if col < nv:
+                sums[unit] = work.tile([P, heads * TILES], F32, name="sums", tag="sums")
+                stats[unit] = work.tile([P, vector_sums(unit), 3], F32, name="stats", tag="stats")
+                squares[unit] = work.tile([P, heads * TILES, DH], BF16, name="squares", tag="squares")
+            for h in range(heads):
+                for j in range(j0, j0 + tiles, 2):
+                    col = h * TILES + j
+                    if col < vector_sums(unit):
                         nc.vector.bn_stats(
-                            out=stats[u][:, col:col + 2, :].rearrange("p a s -> p (a s)"),
+                            out=stats[unit][:, col:col + 2, :].rearrange("p j s -> p (j s)"),
                             in_=stage[c][:, h0 + h, j:j + 2, 1:ROW].rearrange("p j d -> p d j"))
 
         def sums_scalar(s):
-            u, j0, nj = steps[s]
-            c, h0, nh, nv = units[u]
-            for h in range(nh):
-                for j in range(j0, j0 + nj):
-                    col = h * TOK + j
-                    if col >= nv:
-                        nc.scalar.activation(out=squares[u][:, col, :], in_=stage[c][:, h0 + h, j, 1:ROW],
-                                             func=ACT.Square, accum_out=sums[u][:, col:col + 1])
+            unit, j0, tiles = steps[s]
+            c, h0, heads = units[unit]
+            for h in range(heads):
+                for j in range(j0, j0 + tiles):
+                    col = h * TILES + j
+                    if col >= vector_sums(unit):
+                        nc.scalar.activation(out=squares[unit][:, col, :], in_=stage[c][:, h0 + h, j, 1:ROW],
+                                             func=ACT.Square, accum_out=sums[unit][:, col:col + 1])
 
-        def post_mean(u):
-            nc.vector.scalar_tensor_tensor(out=mean_sq[u][:], in0=stats[u][:, :, 1], scalar=float(DH),
-                                           in1=stats[u][:, :, 1], op0=ALU.mult, op1=ALU.mult)
+        def square_means(unit):
+            means = stats[unit][:, :, 1]
+            nc.vector.scalar_tensor_tensor(out=means, in0=means, scalar=float(DH), in1=means,
+                                           op0=ALU.mult, op1=ALU.mult)
 
-        def post_sum(u):
-            nc.vector.tensor_tensor(out=sums[u][:, 0:units[u][3]], in0=mean_sq[u][:], in1=stats[u][:, :, 2], op=ALU.add)
+        def add_stats(unit):
+            nc.vector.tensor_reduce(out=sums[unit][:, 0:vector_sums(unit)], in_=stats[unit][:, :, 1:3],
+                                    axis=mybir.AxisListType.X, op=ALU.add)
 
-        def lift_and_store(u):
-            c, h0, nh, nv = units[u]
-            nc.scalar.activation(out=stage[c][:, h0:h0 + nh, :, 0].rearrange("p h j -> p (h j)"), in_=sums[u][:],
-                                 func=ACT.Sqrt, bias=1.0)
+        def lift_and_store(unit):
+            c, h0, heads = units[unit]
+            nc.scalar.activation(out=stage[c][:, h0:h0 + heads, :, 0].rearrange("p h j -> p (h j)"),
+                                 in_=sums[unit][:], func=ACT.Sqrt, bias=1.0)
             out = out_0 if c < CHUNKS // 2 else out_1
-            view = out.rearrange("b h (g j) c -> h g b (j c)", j=TOK)
-            first = (c % (CHUNKS // 2)) * HEADS
-            for h in range(h0, h0 + nh):
-                nc.sync.dma_start(out=view[first + h], in_=stage[c][:, h].rearrange("p j c -> p (j c)"))
+            runs = out.rearrange("b h (a j) e -> h a b (j e)", j=TILES)
+            for h in range(h0, h0 + heads):
+                nc.sync.dma_start(out=runs[c * HEADS % H + h], in_=stage[c][:, h].rearrange("p j e -> p (j e)"))
 
-        def closes(s):
-            return 0 <= s < STEPS and steps[s][1] + steps[s][2] == TOK
+        def closed_unit(s):
+            if 0 <= s < len(steps) and steps[s][1] + steps[s][2] == TILES:
+                return steps[s][0]
+            return None
 
-        gx = new_grouped()
-        gw = new_grouped()
-        copy_x(transpose_x(0), gx, 0)
-        spread_bias()
-        quantize_x(0, gx, 0, 1)
-        copy_w(transpose_w(0, 0), gw, 0, on_vector=True)
-        copy_w(transpose_w(0, 1), gw, 1)
-        copy_x(transpose_x(1), gx, 1, on_vector=True)
-        quantize_w(0, gw)
-        quantize_x(0, gx, 1, 2)
-        for q in range(1, BANKS):
-            gx = new_grouped()
-            copy_x(transpose_x(2 * q), gx, 0)
-            copy_x(transpose_x(2 * q + 1), gx, 1)
-            multiply(q - 1)
-            add_bias(q - 1)
-            quantize_x(q, gx)
-            if q >= 2:
-                sums_vector(q - 2)
-                sums_scalar(q - 2)
-        gw = new_grouped()
-        copy_w(transpose_w(1, 0), gw, 0)
-        copy_w(transpose_w(1, 1), gw, 1)
-        multiply(BANKS - 1)
-        add_bias(BANKS - 1)
-        quantize_w(1, gw)
-        sums_vector(BANKS - 2)
-        gw = new_grouped()
-        copy_w(transpose_w(2, 0), gw, 0)
-        copy_w(transpose_w(2, 1), gw, 1)
-        sums_scalar(BANKS - 2)
-        for q in range(BANKS):
-            multiply(BANKS + q)
+        grouped_x0 = new_grouped()
+        turn_x(0, grouped_x0, on_vector=False)
+        spread_bq()
+        quantize_x(0, grouped_x0, 0, 1)
+        quantize_w0 = prepare_w(0, vector_pass=0)
+        turn_x(1, grouped_x0, on_vector=True)
+        quantize_w0()
+        quantize_x(0, grouped_x0, 1, 2)
+        prepare_w(1)()
 
-        for s in range(BANKS, STEPS + 3):
-            c, q = divmod(s, BANKS)
-            more = c + 2 < CHUNKS
-            if s < STEPS:
+        plan = {max(1, 2 * q - 2): (lambda q=q: prepare_x(q), max(1, 2 * q - 2)) for q in range(1, TILES // 2)}
+        plan[2 * CHUNK_STEPS - 2] = (lambda: prepare_w(2), 2 * CHUNK_STEPS - 2)
+        for c in range(3, CHUNKS):
+            plan[CHUNK_STEPS * c - WEIGHT_LEAD] = (lambda c=c: prepare_w(c), CHUNK_STEPS * c - WEIGHT_LEAD + 2)
+
+        to_quantize = {}
+        for s in range(len(steps) + 2):
+            if s in plan:
+                prepare, when = plan[s]
+                to_quantize[when] = prepare()
+            ending = closed_unit(s - 2)
+            if s < len(steps):
+                multiply(s)
                 add_bias(s)
-            if s == BANKS:
-                quantize_w(2, gw)
-            if more and q == 0:
-                gw = new_grouped()
-                banks = [transpose_w(c + 2, g) for g in range(PASSES)]
-            if s + BANKS < STEPS:
-                multiply(s + BANKS)
-            if closes(s - 2):
-                post_mean(steps[s - 2][0])
-            if s - 1 < STEPS:
+            if ending is not None:
+                square_means(ending)
+            if s in to_quantize:
+                to_quantize[s]()
+            if 1 <= s <= len(steps):
                 sums_vector(s - 1)
-            if closes(s - 2):
-                post_sum(steps[s - 2][0])
-            if closes(s - 3):
-                lift_and_store(steps[s - 3][0])
-            if s - 1 < STEPS:
+            if ending is not None:
+                add_stats(ending)
+            if 1 <= s <= len(steps):
                 sums_scalar(s - 1)
-            if more and q < PASSES:
-                copy_w(banks[q], gw, q)
-            if more and q == BANKS - 1:
-                quantize_w(c + 2, gw)
+            if ending is not None:
+                lift_and_store(ending)

@@ -29,8 +29,15 @@ CHUNKS = 2 * D // FEATS
 CHUNK_STEPS = TILES * FEATS // BANK
 TRANSPOSE_BANKS, PRODUCT_BANKS = 3, 5
 HALVED_CHUNKS = 2
-VECTOR_EIGHTHS = 3
-WEIGHT_LEAD = 5
+FIRST_CHUNKS = 3
+UNITS_OPEN = FIRST_CHUNKS + 1
+FOLDS = 2
+EARLY_LEAD, LATE_LEAD = 4, 5
+QUANTIZE_LEAD = 3
+FIRST_SHARES = (0, 8, 2, 2)
+FULL_SHARES = (4, 10, 0, 2)
+HALVED_SHARES = (4, 8, 1, 0)
+LAST_SHARES = (4, 8, HEADS // 2, 0)
 
 
 def tile_lorentzmultiheadattention_pa_kernel(tc, x_space, Wq, bq, Wk, bk, out_0, out_1):
@@ -45,6 +52,7 @@ def tile_lorentzmultiheadattention_pa_kernel(tc, x_space, Wq, bq, Wk, bk, out_0,
         nc.gpsimd.memset(bq_rows[:].bitcast(I32), 0)
         ident = keep.tile([P, P], F32, name="ident")
         make_identity(nc, ident[:])
+
         shuffle = keep.tile([P, P], F32, name="shuffle")
         nc.vector.tensor_copy(out=shuffle[:].rearrange("p (a b) -> p a b", b=B),
                               in_=ident[:].rearrange("p (b a) -> p a b", b=B))
@@ -74,10 +82,11 @@ def tile_lorentzmultiheadattention_pa_kernel(tc, x_space, Wq, bq, Wk, bk, out_0,
         nc.sync.dma_start(out=bq_rows[0:2, :], in_=bq.rearrange("(r n) -> r n", r=2))
         load_w(0)
         load_x(1, 1)
-        load_w(1)
+        for c in range(1, FIRST_CHUNKS):
+            load_w(c)
         for j0 in range(2, TILES, 2):
             load_x(j0, 2)
-        for c in range(2, CHUNKS):
+        for c in range(FIRST_CHUNKS, CHUNKS):
             load_w(c)
         bias_k = keep.tile([P, D], BF16, name="bias_k")
         nc.sync.dma_start(out=bias_k[:], in_=bk.partition_broadcast(P))
@@ -154,12 +163,16 @@ def tile_lorentzmultiheadattention_pa_kernel(tc, x_space, Wq, bq, Wk, bk, out_0,
         for unit, (c, h0, heads) in enumerate(units):
             tiles = BANK // (heads * DH)
             steps += [(unit, j0, tiles) for j0 in range(0, TILES, tiles)]
-        steps = [steps[CHUNK_STEPS * c + q] for q in range(CHUNK_STEPS) for c in range(2)] + steps[2 * CHUNK_STEPS:]
+        steps = ([steps[CHUNK_STEPS * c + q] for q in range(CHUNK_STEPS) for c in range(FIRST_CHUNKS)]
+                 + steps[FIRST_CHUNKS * CHUNK_STEPS:])
+        shares = [FIRST_SHARES if c < FIRST_CHUNKS else FULL_SHARES if heads == HEADS else HALVED_SHARES
+                  for c, h0, heads in units[:-1]] + [LAST_SHARES]
 
         products = {}
         sums = {}
         stats = {}
         squares = {}
+        folded = {}
 
         def multiply(s):
             unit, j0, tiles = steps[s]
@@ -187,31 +200,47 @@ def tile_lorentzmultiheadattention_pa_kernel(tc, x_space, Wq, bq, Wk, bk, out_0,
                 in1=bias.unsqueeze(2).to_broadcast([P, heads, tiles, DH]),
                 op=ALU.add)
 
-        def vector_sums(unit):
-            return units[unit][2] * VECTOR_EIGHTHS
-
         def sums_vector(s):
             unit, j0, tiles = steps[s]
             c, h0, heads = units[unit]
+            first, end, pool_head, pool_tile = shares[unit]
             if j0 == 0:
-                sums[unit] = work.tile([P, heads * TILES], F32, name="sums", tag="sums")
-                stats[unit] = work.tile([P, vector_sums(unit), 3], F32, name="stats", tag="stats")
-                squares[unit] = work.tile([P, heads * TILES, DH], BF16, name="squares", tag="squares")
+                sums[unit] = work.tile([P, heads * TILES], F32, name="sums", tag="sums", bufs=UNITS_OPEN)
+                stats[unit] = work.tile([P, end - first, 3], F32, name="stats", tag="stats", bufs=UNITS_OPEN)
+                squares[unit] = work.tile([P, heads * TILES, DH], BF16, name="squares", tag="squares", bufs=UNITS_OPEN)
             for h in range(heads):
                 for j in range(j0, j0 + tiles, 2):
                     col = h * TILES + j
-                    if col < vector_sums(unit):
+                    if first <= col < end:
                         nc.vector.bn_stats(
-                            out=stats[unit][:, col:col + 2, :].rearrange("p j s -> p (j s)"),
+                            out=stats[unit][:, col - first:col - first + 2, :].rearrange("p j s -> p (j s)"),
                             in_=stage[c][:, h0 + h, j:j + 2, 1:ROW].rearrange("p j d -> p d j"))
+
+        def sums_gpsimd(s):
+            unit, j0, tiles = steps[s]
+            c, h0, heads = units[unit]
+            first, end, pool_head, pool_tile = shares[unit]
+            if j0 != pool_tile or pool_head == heads:
+                return
+            values = stage[c][:, h0 + pool_head:h0 + heads, j0:j0 + tiles, 1:ROW]
+            part = work.tile([P, heads - pool_head, tiles, DH], F32, name="pool_squares", tag="pool_squares")
+            nc.gpsimd.tensor_tensor(out=part[:], in0=values, in1=values, op=ALU.mult)
+            for fold in range(1, FOLDS + 1):
+                width = DH >> fold
+                half = work.tile([P, heads - pool_head, tiles, width], F32, name="fold", tag="fold%d" % fold)
+                nc.gpsimd.tensor_tensor(out=half[:], in0=part[:, :, :, 0:width], in1=part[:, :, :, width:2 * width],
+                                        op=ALU.add)
+                part = half
+            folded[unit] = part
 
         def sums_scalar(s):
             unit, j0, tiles = steps[s]
             c, h0, heads = units[unit]
-            for h in range(heads):
+            first, end, pool_head, pool_tile = shares[unit]
+            for h in range(pool_head if j0 == pool_tile else heads):
                 for j in range(j0, j0 + tiles):
                     col = h * TILES + j
-                    if col >= vector_sums(unit):
+                    if not first <= col < end:
                         nc.scalar.activation(out=squares[unit][:, col, :], in_=stage[c][:, h0 + h, j, 1:ROW],
                                              func=ACT.Square, accum_out=sums[unit][:, col:col + 1])
 
@@ -220,8 +249,14 @@ def tile_lorentzmultiheadattention_pa_kernel(tc, x_space, Wq, bq, Wk, bk, out_0,
             nc.vector.scalar_tensor_tensor(out=means, in0=means, scalar=float(DH), in1=means,
                                            op0=ALU.mult, op1=ALU.mult)
 
-        def add_stats(unit):
-            nc.vector.tensor_reduce(out=sums[unit][:, 0:vector_sums(unit)], in_=stats[unit][:, :, 1:3],
+        def finish_sums(unit):
+            first, end, pool_head, pool_tile = shares[unit]
+            if unit in folded:
+                tiles = folded[unit].shape[2]
+                by_head = sums[unit][:].rearrange("p (h j) -> p h j", j=TILES)
+                nc.vector.tensor_reduce(out=by_head[:, pool_head:, pool_tile:pool_tile + tiles], in_=folded[unit][:],
+                                        axis=mybir.AxisListType.X, op=ALU.add)
+            nc.vector.tensor_reduce(out=sums[unit][:, first:end], in_=stats[unit][:, :, 1:3],
                                     axis=mybir.AxisListType.X, op=ALU.add)
 
         def lift_and_store(unit):
@@ -247,13 +282,17 @@ def tile_lorentzmultiheadattention_pa_kernel(tc, x_space, Wq, bq, Wk, bk, out_0,
         quantize_w0()
         quantize_x(0, grouped_x0, 1, 2)
         prepare_w(1)()
+        to_quantize = {0: prepare_w(2)}
 
-        plan = {max(1, 2 * q - 2): (lambda q=q: prepare_x(q), max(1, 2 * q - 2)) for q in range(1, TILES // 2)}
-        plan[2 * CHUNK_STEPS - 2] = (lambda: prepare_w(2), 2 * CHUNK_STEPS - 2)
-        for c in range(3, CHUNKS):
-            plan[CHUNK_STEPS * c - WEIGHT_LEAD] = (lambda c=c: prepare_w(c), CHUNK_STEPS * c - WEIGHT_LEAD + 2)
+        plan = {}
+        for q in range(1, TILES // 2):
+            needed = FIRST_CHUNKS * q
+            plan[max(1, needed - EARLY_LEAD)] = (lambda q=q: prepare_x(q), max(1, needed - QUANTIZE_LEAD))
+        for c in range(FIRST_CHUNKS, CHUNKS):
+            needed = CHUNK_STEPS * c
+            lead = EARLY_LEAD if c == FIRST_CHUNKS else LATE_LEAD
+            plan[needed - lead] = (lambda c=c: prepare_w(c), needed - QUANTIZE_LEAD)
 
-        to_quantize = {}
         for s in range(len(steps) + 2):
             if s in plan:
                 prepare, when = plan[s]
@@ -268,8 +307,9 @@ def tile_lorentzmultiheadattention_pa_kernel(tc, x_space, Wq, bq, Wk, bk, out_0,
                 to_quantize[s]()
             if 1 <= s <= len(steps):
                 sums_vector(s - 1)
+                sums_gpsimd(s - 1)
             if ending is not None:
-                add_stats(ending)
+                finish_sums(ending)
             if 1 <= s <= len(steps):
                 sums_scalar(s - 1)
             if ending is not None:

@@ -29,12 +29,12 @@ CHUNKS = 2 * D // FEATS
 CHUNK_STEPS = TILES * FEATS // BANK
 TRANSPOSE_BANKS, PRODUCT_BANKS = 3, 5
 HALVED_CHUNKS = 2
-FIRST_CHUNKS = 3
+FIRST_CHUNKS = 2
 UNITS_OPEN = FIRST_CHUNKS + 1
 FOLDS = 2
-EARLY_LEAD, LATE_LEAD = 4, 5
+EARLY_LEAD, LATE_LEAD = 3, 5
 QUANTIZE_LEAD = 3
-FIRST_SHARES = (0, 8, 2, 2)
+FIRST_SHARES = (0, 10, HEADS, 0)
 FULL_SHARES = (4, 10, 0, 2)
 HALVED_SHARES = (4, 8, 1, 0)
 LAST_SHARES = (4, 8, HEADS // 2, 0)
@@ -282,17 +282,17 @@ def tile_lorentzmultiheadattention_pa_kernel(tc, x_space, Wq, bq, Wk, bk, out_0,
         quantize_w0()
         quantize_x(0, grouped_x0, 1, 2)
         prepare_w(1)()
-        to_quantize = {0: prepare_w(2)}
 
         plan = {}
         for q in range(1, TILES // 2):
             needed = FIRST_CHUNKS * q
-            plan[max(1, needed - EARLY_LEAD)] = (lambda q=q: prepare_x(q), max(1, needed - QUANTIZE_LEAD))
+            plan[max(0, needed - EARLY_LEAD)] = (lambda q=q: prepare_x(q), max(0, needed - QUANTIZE_LEAD))
         for c in range(FIRST_CHUNKS, CHUNKS):
             needed = CHUNK_STEPS * c
             lead = EARLY_LEAD if c == FIRST_CHUNKS else LATE_LEAD
             plan[needed - lead] = (lambda c=c: prepare_w(c), needed - QUANTIZE_LEAD)
 
+        to_quantize = {}
         for s in range(len(steps) + 2):
             if s in plan:
                 prepare, when = plan[s]

from contextlib import ExitStack

import concourse.mybir as mybir
from concourse.masks import make_identity

B, N, DI, D, H = 2, 512, 1024, 1024, 16
DH = D // H
FLOPS = 2 * B * N * DI * 2 * D

F32 = mybir.dt.float32
BF16 = mybir.dt.bfloat16
I32 = mybir.dt.int32
U32 = mybir.dt.uint32
U8 = mybir.dt.uint8
E4M3 = mybir.dt.float8_e4m3fn_x4
E5M2 = mybir.dt.float8_e5m2_x4
ALU = mybir.AluOpType
ACT = mybir.ActivationFunctionType

P = 128
BANK = 512
TILES = 8
PASSES = 2
PASS_PAIRS = 256
ROW = DH + 1
HEADS = 4
FEATS = HEADS * DH
CHUNKS = 2 * D // FEATS
CHUNK_STEPS = TILES * FEATS // BANK
TRANSPOSE_BANKS, PRODUCT_BANKS = 3, 5
HALVED_CHUNKS = 2
FIRST_CHUNKS = 2
UNITS_OPEN = FIRST_CHUNKS + 1
FOLDS = 2
EARLY_LEAD, LATE_LEAD = 3, 5
QUANTIZE_LEAD = 3
FIRST_SHARES = (0, 10, HEADS, 0)
FULL_SHARES = (4, 10, 0, 2)
HALVED_SHARES = (4, 8, 1, 0)
LAST_SHARES = (4, 8, HEADS // 2, 0)


def tile_lorentzmultiheadattention_pa_kernel(tc, x_space, Wq, bq, Wk, bk, out_0, out_1):
    nc = tc.nc
    with ExitStack() as ctx:
        keep = ctx.enter_context(tc.tile_pool(name="keep", bufs=1))
        work = ctx.enter_context(tc.tile_pool(name="work", bufs=3))
        psum = ctx.enter_context(tc.psum_pool(name="psum", bufs=1))
        ctx.enter_context(tc.manual_schedule())

        bq_rows = keep.tile([P, BANK], BF16, name="bq_rows")
        nc.gpsimd.memset(bq_rows[:].bitcast(I32), 0)
        ident = keep.tile([P, P], F32, name="ident")
        make_identity(nc, ident[:])

        shuffle = keep.tile([P, P], F32, name="shuffle")
        nc.vector.tensor_copy(out=shuffle[:].rearrange("p (a b) -> p a b", b=B),
                              in_=ident[:].rearrange("p (b a) -> p a b", b=B))

        def every_second_pair(row):
            pairs = row.bitcast(F32)
            return [[pairs[:, PASS_PAIRS * g + u:PASS_PAIRS * (g + 1):2] for u in range(2)] for g in range(PASSES)]

        x_rows = x_space.rearrange("b (a j) k -> (b a) j k", j=TILES)
        x_pairs = {}
        w_pairs = {}

        def load_x(j0, count):
            raw = keep.tile([P, count, DI], BF16, name="x_raw%d" % j0)
            nc.sync.dma_start(out=raw[:], in_=x_rows[:, j0:j0 + count, :])
            for j in range(count):
                x_pairs[j0 + j] = every_second_pair(raw[:, j, :])

        def load_w(c):
            weights = Wq if c < CHUNKS // 2 else Wk
            f0 = c * FEATS % D
            raw = keep.tile([P, 2, DI], BF16, name="w_raw%d" % c)
            nc.sync.dma_start(out=raw[:], in_=weights[f0:f0 + FEATS, :].rearrange("(r i) k -> r i k", i=2))
            w_pairs[c] = [every_second_pair(raw[:, i, :]) for i in range(2)]

        load_x(0, 1)
        nc.sync.dma_start(out=bq_rows[0:2, :], in_=bq.rearrange("(r n) -> r n", r=2))
        load_w(0)
        load_x(1, 1)
        for c in range(1, FIRST_CHUNKS):
            load_w(c)
        for j0 in range(2, TILES, 2):
            load_x(j0, 2)
        for c in range(FIRST_CHUNKS, CHUNKS):
            load_w(c)
        bias_k = keep.tile([P, D], BF16, name="bias_k")
        nc.sync.dma_start(out=bias_k[:], in_=bk.partition_broadcast(P))

        select = keep.tile([P, 2], BF16, name="select")
        nc.scalar.activation(out=select[:], in_=ident[:, 0:2], func=ACT.Sqrt)
        bias_q = keep.tile([P, D], BF16, name="bias_q")

        def spread_bq():
            bank = psum.tile([P, 2, BANK], BF16, name="bq_bank", tag="product", bufs=PRODUCT_BANKS)
            for r in range(2):
                nc.tensor.matmul(bank[:, r, :], lhsT=select[:, r:r + 1].to_broadcast([P, P]), rhs=bq_rows[:],
                                 start=True, stop=True)
            nc.scalar.copy(out=bias_q[:], in_=bank[:].rearrange("p r n -> p (r n)"))

        x_codes = [keep.tile([P, 2, PASSES, P], U32, name="x_codes%d" % q, align_bytes=64) for q in range(TILES // 2)]
        x_scales = [keep.tile([P, 2, PASSES, P], U8, name="x_scales%d" % q, align_bytes=64) for q in range(TILES // 2)]
        w_codes = [keep.tile([P, PASSES, FEATS], U32, name="w_codes%d" % c, align_bytes=64) for c in range(CHUNKS)]
        w_scales = [keep.tile([P, PASSES, FEATS], U8, name="w_scales%d" % c, align_bytes=64) for c in range(CHUNKS)]
        stage = [keep.tile([P, HEADS, TILES, ROW], F32, name="stage%d" % c) for c in range(CHUNKS)]

        def new_grouped():
            return work.tile([P, 2, BANK], F32, name="grouped", tag="grouped", bufs=4, align_bytes=64)

        def copy(on_vector, out, in_):
            if on_vector:
                nc.vector.tensor_copy(out=out, in_=in_)
            else:
                nc.scalar.copy(out=out, in_=in_)

        def turn_x(j, grouped, on_vector):
            bank = psum.tile([P, PASSES, 2, P], F32, name="x_bank", tag="transpose", bufs=TRANSPOSE_BANKS)
            for g in range(PASSES):
                for u in range(2):
                    nc.tensor.transpose(bank[:, g, u, :], x_pairs[j][g][u], shuffle[:])
            copy(on_vector, grouped[:, j % 2, :].rearrange("p (g m u) -> p g m u", g=PASSES, u=2),
                 bank[:].rearrange("p g u m -> p g m u"))

        def turn_w(c, g, grouped, on_vector):
            bank = psum.tile([P, 2, 2, P], F32, name="w_bank", tag="transpose", bufs=TRANSPOSE_BANKS)
            for i in range(2):
                for u in range(2):
                    nc.tensor.transpose(bank[:, i, u, :], w_pairs[c][i][g][u], ident[:])
            copy(on_vector, grouped[:, g, :].rearrange("p (r iu) -> p r iu", iu=4),
                 bank[:].rearrange("p i u r -> p r (i u)"))

        def quantize_x(q, grouped, lo, hi):
            nc.vector.quantize_mx(
                out=x_codes[q][:, lo:hi].rearrange("p j g m -> p (j g m)").bitcast(E5M2),
                scales=x_scales[q][:, lo:hi].rearrange("p j g m -> p (j g m)"),
                in_=grouped[:, lo:hi, :].rearrange("p j w -> p (j w)").bitcast(BF16))

        def quantize_w(c, grouped):
            nc.vector.quantize_mx(
                out=w_codes[c][:].rearrange("p g n -> p (g n)").bitcast(E4M3),
                scales=w_scales[c][:].rearrange("p g n -> p (g n)"),
                in_=grouped[:].rearrange("p g w -> p (g w)").bitcast(BF16))

        def prepare_x(q):
            grouped = new_grouped()
            for j in (2 * q, 2 * q + 1):
                turn_x(j, grouped, on_vector=False)
            return lambda: quantize_x(q, grouped, 0, 2)

        def prepare_w(c, vector_pass=None):
            grouped = new_grouped()
            for g in range(PASSES):
                turn_w(c, g, grouped, on_vector=g == vector_pass)
            return lambda: quantize_w(c, grouped)

        units = [(c, 0, HEADS) for c in range(CHUNKS - HALVED_CHUNKS)]
        units += [(c, h0, HEADS // 2) for c in range(CHUNKS - HALVED_CHUNKS, CHUNKS) for h0 in (0, HEADS // 2)]
        steps = []
        for unit, (c, h0, heads) in enumerate(units):
            tiles = BANK // (heads * DH)
            steps += [(unit, j0, tiles) for j0 in range(0, TILES, tiles)]
        steps = ([steps[CHUNK_STEPS * c + q] for q in range(CHUNK_STEPS) for c in range(FIRST_CHUNKS)]
                 + steps[FIRST_CHUNKS * CHUNK_STEPS:])
        shares = [FIRST_SHARES if c < FIRST_CHUNKS else FULL_SHARES if heads == HEADS else HALVED_SHARES
                  for c, h0, heads in units[:-1]] + [LAST_SHARES]

        products = {}
        sums = {}
        stats = {}
        squares = {}
        folded = {}

        def multiply(s):
            unit, j0, tiles = steps[s]
            c, h0, heads = units[unit]
            cols = slice(h0 * DH, (h0 + heads) * DH)
            bank = psum.tile([P, tiles, heads * DH], F32, name="product_bank", tag="product", bufs=PRODUCT_BANKS)
            for jj in range(tiles):
                q, half = divmod(j0 + jj, 2)
                for g in range(PASSES):
                    nc.tensor.matmul_mx(
                        out=bank[:, jj, :],
                        lhsT=x_codes[q][:, half, g, :].bitcast(E5M2), lhsT_scale=x_scales[q][:, half, g, :],
                        rhs=w_codes[c][:, g, cols].bitcast(E4M3), rhs_scale=w_scales[c][:, g, cols],
                        start=(g == 0), stop=(g == PASSES - 1))
            products[s] = bank

        def add_bias(s):
            unit, j0, tiles = steps[s]
            c, h0, heads = units[unit]
            f0 = c * FEATS % D + h0 * DH
            bias = (bias_q if c < CHUNKS // 2 else bias_k)[:, f0:f0 + heads * DH].rearrange("p (h d) -> p h d", d=DH)
            nc.vector.tensor_tensor(
                out=stage[c][:, h0:h0 + heads, j0:j0 + tiles, 1:ROW],
                in0=products[s][:].rearrange("p j (h d) -> p h j d", d=DH),
                in1=bias.unsqueeze(2).to_broadcast([P, heads, tiles, DH]),
                op=ALU.add)

        def sums_vector(s):
            unit, j0, tiles = steps[s]
            c, h0, heads = units[unit]
            first, end, pool_head, pool_tile = shares[unit]
            if j0 == 0:
                sums[unit] = work.tile([P, heads * TILES], F32, name="sums", tag="sums", bufs=UNITS_OPEN)
                stats[unit] = work.tile([P, end - first, 3], F32, name="stats", tag="stats", bufs=UNITS_OPEN)
                squares[unit] = work.tile([P, heads * TILES, DH], BF16, name="squares", tag="squares", bufs=UNITS_OPEN)
            for h in range(heads):
                for j in range(j0, j0 + tiles, 2):
                    col = h * TILES + j
                    if first <= col < end:
                        nc.vector.bn_stats(
                            out=stats[unit][:, col - first:col - first + 2, :].rearrange("p j s -> p (j s)"),
                            in_=stage[c][:, h0 + h, j:j + 2, 1:ROW].rearrange("p j d -> p d j"))

        def sums_gpsimd(s):
            unit, j0, tiles = steps[s]
            c, h0, heads = units[unit]
            first, end, pool_head, pool_tile = shares[unit]
            if j0 != pool_tile or pool_head == heads:
                return
            values = stage[c][:, h0 + pool_head:h0 + heads, j0:j0 + tiles, 1:ROW]
            part = work.tile([P, heads - pool_head, tiles, DH], F32, name="pool_squares", tag="pool_squares")
            nc.gpsimd.tensor_tensor(out=part[:], in0=values, in1=values, op=ALU.mult)
            for fold in range(1, FOLDS + 1):
                width = DH >> fold
                half = work.tile([P, heads - pool_head, tiles, width], F32, name="fold", tag="fold%d" % fold)
                nc.gpsimd.tensor_tensor(out=half[:], in0=part[:, :, :, 0:width], in1=part[:, :, :, width:2 * width],
                                        op=ALU.add)
                part = half
            folded[unit] = part

        def sums_scalar(s):
            unit, j0, tiles = steps[s]
            c, h0, heads = units[unit]
            first, end, pool_head, pool_tile = shares[unit]
            for h in range(pool_head if j0 == pool_tile else heads):
                for j in range(j0, j0 + tiles):
                    col = h * TILES + j
                    if not first <= col < end:
                        nc.scalar.activation(out=squares[unit][:, col, :], in_=stage[c][:, h0 + h, j, 1:ROW],
                                             func=ACT.Square, accum_out=sums[unit][:, col:col + 1])

        def square_means(unit):
            means = stats[unit][:, :, 1]
            nc.vector.scalar_tensor_tensor(out=means, in0=means, scalar=float(DH), in1=means,
                                           op0=ALU.mult, op1=ALU.mult)

        def finish_sums(unit):
            first, end, pool_head, pool_tile = shares[unit]
            if unit in folded:
                tiles = folded[unit].shape[2]
                by_head = sums[unit][:].rearrange("p (h j) -> p h j", j=TILES)
                nc.vector.tensor_reduce(out=by_head[:, pool_head:, pool_tile:pool_tile + tiles], in_=folded[unit][:],
                                        axis=mybir.AxisListType.X, op=ALU.add)
            nc.vector.tensor_reduce(out=sums[unit][:, first:end], in_=stats[unit][:, :, 1:3],
                                    axis=mybir.AxisListType.X, op=ALU.add)

        def lift_and_store(unit):
            c, h0, heads = units[unit]
            nc.scalar.activation(out=stage[c][:, h0:h0 + heads, :, 0].rearrange("p h j -> p (h j)"),
                                 in_=sums[unit][:], func=ACT.Sqrt, bias=1.0)
            out = out_0 if c < CHUNKS // 2 else out_1
            runs = out.rearrange("b h (a j) e -> h a b (j e)", j=TILES)
            for h in range(h0, h0 + heads):
                nc.sync.dma_start(out=runs[c * HEADS % H + h], in_=stage[c][:, h].rearrange("p j e -> p (j e)"))

        def closed_unit(s):
            if 0 <= s < len(steps) and steps[s][1] + steps[s][2] == TILES:
                return steps[s][0]
            return None

        grouped_x0 = new_grouped()
        turn_x(0, grouped_x0, on_vector=False)
        spread_bq()
        quantize_x(0, grouped_x0, 0, 1)
        quantize_w0 = prepare_w(0, vector_pass=0)
        turn_x(1, grouped_x0, on_vector=True)
        quantize_w0()
        quantize_x(0, grouped_x0, 1, 2)
        prepare_w(1)()

        plan = {}
        for q in range(1, TILES // 2):
            needed = FIRST_CHUNKS * q
            plan[max(0, needed - EARLY_LEAD)] = (lambda q=q: prepare_x(q), max(0, needed - QUANTIZE_LEAD))
        for c in range(FIRST_CHUNKS, CHUNKS):
            needed = CHUNK_STEPS * c
            lead = EARLY_LEAD if c == FIRST_CHUNKS else LATE_LEAD
            plan[needed - lead] = (lambda c=c: prepare_w(c), needed - QUANTIZE_LEAD)

        to_quantize = {}
        for s in range(len(steps) + 2):
            if s in plan:
                prepare, when = plan[s]
                to_quantize[when] = prepare()
            ending = closed_unit(s - 2)
            if s < len(steps):
                multiply(s)
                add_bias(s)
            if ending is not None:
                square_means(ending)
            if s in to_quantize:
                to_quantize[s]()
            if 1 <= s <= len(steps):
                sums_vector(s - 1)
                sums_gpsimd(s - 1)
            if ending is not None:
                finish_sums(ending)
            if 1 <= s <= len(steps):
                sums_scalar(s - 1)
            if ending is not None:
                lift_and_store(ending)
